import numpy as np
import ml_dtypes


def mxq(x, axis, fmt="e4m3"):
    dtype, down = {"e4m3": (ml_dtypes.float8_e4m3fn, 7), "e5m2": (ml_dtypes.float8_e5m2, 14)}[fmt]
    v = np.moveaxis(np.asarray(x, np.float32).astype(ml_dtypes.bfloat16).astype(np.float64), axis, -1)
    blocks = v.reshape(v.shape[:-1] + (-1, 32))
    amax = np.abs(blocks).max(-1, keepdims=True)
    byte = np.maximum(np.where(amax > 0, np.frexp(amax)[1] - 1 + 127, 0) - down, 1)
    scale = np.exp2(byte - 127.0)
    codes = (blocks / scale).astype(np.float32).astype(dtype).astype(np.float64)
    return np.moveaxis((codes * scale).reshape(v.shape), -1, axis)


WIDE = False


def mx_kscale(k):
    if not WIDE:
        return np.ones(k)
    levels = np.array([10, -10, 5, -5, 0])
    a = np.random.permutation(np.resize(levels, k // 512 * 4)).reshape(k // 512, 4)
    idx = np.arange(k)
    return np.exp2(a[idx // 512, idx % 128 // 32])


BF16 = ml_dtypes.bfloat16


def bf(x):
    return np.asarray(x, np.float32).astype(BF16)


def f64(x):
    return np.asarray(x).astype(np.float64)


E2M1 = np.array([0.0, 0.5, 1.0, 1.5, 2.0, 3.0, 4.0, 6.0, -0.0, -0.5, -1.0, -1.5, -2.0, -3.0, -4.0, -6.0])


def pack_weight(w, fmt):
    k, n = w.shape
    w = f64(bf(w)).reshape(k // 32, 32, n)
    amax = np.abs(w).max(1)
    if fmt == "e4m3":
        byte = np.frexp(amax)[1] - 1 + 127 - 7
    else:
        mant, ex = np.frexp(amax / 6.0)
        byte = np.where(mant > 0.5, ex, ex - 1) + 127
    byte = np.clip(np.where(amax > 0, byte, 1), 1, 254)
    scaled = (w * np.exp2(127.0 - byte)[:, None, :]).reshape(k, n).astype(np.float32)
    by_word = np.ascontiguousarray(scaled.reshape(k // 512, 128, 4, n).transpose(0, 1, 3, 2))
    if fmt == "e4m3":
        words = by_word.astype(ml_dtypes.float8_e4m3fn).view(np.uint8)
    else:
        c = by_word.astype(ml_dtypes.float4_e2m1fn).view(np.uint8) & 0xF
        words = c[..., 0::2] | (c[..., 1::2] << 4)
    return np.ascontiguousarray(words), np.ascontiguousarray(byte.astype(np.uint8).reshape(k // 512, 16, n))


def unpack_weight(words, scales, fmt):
    g, p, n, _ = words.shape
    if fmt == "e4m3":
        vals = np.ascontiguousarray(words).view(ml_dtypes.float8_e4m3fn).astype(np.float64)
    else:
        nib = np.empty((g, p, n, 4), np.uint8)
        nib[..., 0::2] = words & 0xF
        nib[..., 1::2] = words >> 4
        vals = E2M1[nib]
    vals = vals * np.repeat(np.exp2(scales.astype(np.float64) - 127.0), 8, axis=1)[..., None]
    return vals.transpose(0, 1, 3, 2).reshape(g * 512, n)

def pack4(w):
    words, scales = pack_weight(w, "e2m1")
    return words.reshape(words.shape[0], 128, -1), scales


def unpack4(words, scales):
    return unpack_weight(words.reshape(words.shape[0], 128, -1, 2), scales, "e2m1")


B, N, D, H = 8, 16, 128, 16384


def setup_inputs():
    t = mx_kscale(H)
    xi_p = bf(np.random.standard_normal((B, N, H)) * 0.7 * t)
    xj_p = bf(np.random.standard_normal((B, N, H)) * 0.7 * t)
    node_mask = bf(np.random.uniform(size=(B, N)) < 0.9)
    mb1 = bf(np.random.standard_normal(H) * 0.2 * t)
    mw2_words, mw2_scales = pack4(np.random.standard_normal((H, D)) * 0.5 / np.sqrt(H) / t[:, None])
    mb2 = bf(np.random.standard_normal(D) * 0.1)
    return {
        "xi_p": xi_p,
        "xj_p": xj_p,
        "node_mask": node_mask,
        "mb1": mb1,
        "mw2_words": mw2_words,
        "mw2_scales": mw2_scales,
        "mb2": mb2,
    }


def reference(xi_p, xj_p, node_mask, mb1, mw2_words, mw2_scales, mb2):
    mask = f64(node_mask)[..., None]
    h = np.maximum(f64(xi_p)[:, :, None, :] + f64(xj_p)[:, None, :, :] + f64(mb1), 0.0)
    msgs = np.maximum((mxq(h, 3, "e4m3") @ unpack4(mw2_words, mw2_scales)) + f64(mb2), 0.0)
    msgs = msgs * mask[:, None]
    return msgs.sum(axis=2)

@@ -1,0 +1,228 @@
+from contextlib import ExitStack
+
+import concourse.mybir as mybir
+from concourse.masks import make_identity
+
+F32 = mybir.dt.float32
+BF16 = mybir.dt.bfloat16
+I32 = mybir.dt.int32
+U32 = mybir.dt.uint32
+U8 = mybir.dt.uint8
+FP8X4 = mybir.dt.float8_e4m3fn_x4
+FP4X4 = mybir.dt.float4_e2m1fn_x4
+ADD = mybir.AluOpType.add
+MULT = mybir.AluOpType.mult
+ACT = mybir.ActivationFunctionType
+
+P = 128
+PACK = 4
+K_PASS = P * PACK
+GRAPHS = 8
+NODES = 16
+HIDDEN = 16384
+D_OUT = 128
+PASSES = HIDDEN // K_PASS
+NODE_ROWS = GRAPHS * NODES
+CHUNK_GRAPHS = 2
+CHUNK_PAIRS = CHUNK_GRAPHS * NODES * NODES
+CHUNK_NODES = CHUNK_GRAPHS * NODES
+CHUNKS = GRAPHS // CHUNK_GRAPHS
+LOAD_PASSES = 4
+LOAD_COLS = LOAD_PASSES * K_PASS
+LAG = 2
+
+FLOPS = 2 * GRAPHS * NODES * NODES * HIDDEN * D_OUT
+
+
+def tile_graphdynamics_pa_k_kernel(
+    tc, xi_p, xj_p, node_mask, mb1, mw2_words, mw2_scales, mb2, out
+):
+    nc = tc.nc
+    with ExitStack() as stack:
+        keep = stack.enter_context(tc.tile_pool(name="keep", bufs=1))
+        loads = stack.enter_context(tc.tile_pool(name="loads", bufs=3))
+        turned_sb = stack.enter_context(tc.tile_pool(name="turned_sb", bufs=2))
+        work = stack.enter_context(tc.tile_pool(name="work", bufs=4))
+        sums_ps = stack.enter_context(tc.psum_pool(name="sums_ps", bufs=1))
+        turn_ps = stack.enter_context(tc.psum_pool(name="turn_ps", bufs=2))
+
+        xi_rows = xi_p.rearrange("b n h -> (b n) h")
+        xj_rows = xj_p.rearrange("b n h -> (b n) h")
+        x_tiles = {}
+
+        def load_x(group):
+            cols = slice(group * LOAD_COLS, (group + 1) * LOAD_COLS)
+            xi_sb = loads.tile([P, LOAD_COLS], BF16, name="xi_sb")
+            nc.sync.dma_start(out=xi_sb[:], in_=xi_rows[:, cols])
+            xj_sb = loads.tile([P, LOAD_COLS], BF16, name="xj_sb")
+            nc.sync.dma_start(out=xj_sb[:], in_=xj_rows[:, cols])
+            x_tiles[group] = (xi_sb, xj_sb)
+
+        load_x(0)
+
+        ident_bf = keep.tile([P, P], BF16, name="ident_bf")
+        make_identity(nc, ident_bf[:])
+        ident_f32 = keep.tile([P, P], F32, name="ident_f32")
+        make_identity(nc, ident_f32[:])
+
+        w_scales = keep.tile([P, PASSES, D_OUT], U8, name="w_scales", align_bytes=64)
+        nc.vector.memset(w_scales[:].bitcast(I32), 0)
+        scale_words = mw2_scales.bitcast(I32)
+        for quadrant in range(4):
+            nc.sync.dma_start(
+                out=w_scales[32 * quadrant : 32 * quadrant + 4].bitcast(I32),
+                in_=scale_words[:, 4 * quadrant : 4 * quadrant + 4, :].rearrange("g r n -> r g n"),
+            )
+        w_codes = keep.tile([P, PASSES, 2 * D_OUT], U8, name="w_codes", align_bytes=64)
+        nc.sync.dma_start(
+            out=w_codes[:].bitcast(I32), in_=mw2_words.bitcast(I32).rearrange("g p c -> p g c")
+        )
+
+        mb1_rows = keep.tile([P, K_PASS], BF16, name="mb1_rows")
+        nc.vector.memset(mb1_rows[:], 0.0)
+        nc.scalar.dma_start(out=mb1_rows[0:PASSES, :], in_=mb1.rearrange("(g c) -> g c", c=K_PASS))
+        mb2_rows = keep.tile([P, D_OUT], BF16, name="mb2_rows")
+        nc.vector.memset(mb2_rows[:], 0.0)
+        nc.scalar.dma_start(out=mb2_rows[0:1, :], in_=mb2.rearrange("(o d) -> o d", o=1))
+        mask_all = keep.tile([P, NODE_ROWS], BF16, name="mask_all")
+        nc.scalar.dma_start(
+            out=mask_all[:], in_=node_mask.rearrange("b n -> (b n)").partition_broadcast(P)
+        )
+        bias_ps = turn_ps.tile([P, PACK + 1, P], BF16, name="bias_ps", tag="turned_i")
+        for t in range(PACK):
+            nc.tensor.transpose(bias_ps[:, t, :], mb1_rows[:, t:K_PASS:PACK], ident_bf[:])
+        nc.tensor.transpose(bias_ps[:, PACK, :], mb2_rows[:], ident_bf[:])
+        mb1_col = keep.tile([P, PACK, PASSES], F32, name="mb1_col")
+        nc.vector.tensor_copy(out=mb1_col[:], in_=bias_ps[:, 0:PACK, 0:PASSES])
+        mb2_col = keep.tile([P, 1], F32, name="mb2_col")
+        nc.vector.tensor_copy(out=mb2_col[:], in_=bias_ps[:, PACK, 0:1])
+
+        sums = [
+            sums_ps.tile([P, CHUNK_PAIRS], F32, name="sums%d" % c) for c in range(CHUNKS)
+        ]
+
+        turned = {}
+
+        def turn_pass(g):
+            group, local = divmod(g, LOAD_PASSES)
+            if local == 0 and group + 1 < PASSES // LOAD_PASSES:
+                load_x(group + 1)
+            xi_sb, xj_sb = x_tiles[group]
+            turned_i = turn_ps.tile([P, PACK, NODE_ROWS], BF16, name="turned_i")
+            for t in range(PACK):
+                nc.tensor.transpose(
+                    turned_i[:, t, :],
+                    xi_sb[:, local * K_PASS + t : (local + 1) * K_PASS : PACK],
+                    ident_bf[:],
+                )
+            recv = turned_sb.tile([P, PACK, NODE_ROWS], F32, name="recv")
+            for t in range(PACK):
+                nc.scalar.activation(
+                    out=recv[:, t, :],
+                    in_=turned_i[:, t, :],
+                    func=ACT.Identity,
+                    bias=mb1_col[:, t, g : g + 1],
+                    scale=1.0,
+                )
+            words = K_PASS // 2
+            xj_words = xj_sb[:].bitcast(F32)
+            turned_j = turn_ps.tile([P, NODE_ROWS, 2], F32, name="turned_j")
+            for u in range(2):
+                nc.tensor.transpose(
+                    turned_j[:, :, u],
+                    xj_words[:, local * words + u : (local + 1) * words : 2],
+                    ident_f32[:],
+                )
+            turned[g] = (recv, turned_j)
+
+        hidden = {}
+
+        def add_and_relu(g, c):
+            recv, turned_j = turned[g]
+            shape = [P, CHUNK_GRAPHS, NODES, NODES, PACK]
+            recv_view = (
+                recv[:, :, c * CHUNK_NODES : (c + 1) * CHUNK_NODES]
+                .rearrange("p t (b i) -> p b i t", b=CHUNK_GRAPHS)
+                .unsqueeze(3)
+                .to_broadcast(shape)
+            )
+            send_view = (
+                turned_j[:]
+                .rearrange("p r u -> p (r u)")
+                .bitcast(BF16)
+                .rearrange("p (b j t) -> p b j t", b=GRAPHS, j=NODES)[
+                    :, c * CHUNK_GRAPHS : (c + 1) * CHUNK_GRAPHS
+                ]
+                .unsqueeze(2)
+                .to_broadcast(shape)
+            )
+            pre = work.tile([P, CHUNK_PAIRS * PACK], BF16, name="pre")
+            nc.vector.tensor_tensor(
+                out=pre[:].rearrange(
+                    "p (b i j t) -> p b i j t", b=CHUNK_GRAPHS, i=NODES, j=NODES
+                ),
+                in0=recv_view,
+                in1=send_view,
+                op=ADD,
+            )
+            h = work.tile([P, CHUNK_PAIRS * PACK], BF16, name="h", align_bytes=64)
+            nc.scalar.activation(out=h[:], in_=pre[:], func=ACT.Relu)
+            hidden[(g, c)] = h
+
+        def quantise_and_multiply(g, c):
+            h = hidden[(g, c)]
+            h_codes = work.tile([P, CHUNK_PAIRS], U32, name="h_codes", align_bytes=64)
+            h_scales = work.tile([P, CHUNK_PAIRS], U8, name="h_scales", align_bytes=64)
+            nc.vector.quantize_mx(out=h_codes[:].bitcast(FP8X4), scales=h_scales[:], in_=h[:])
+            nc.tensor.matmul_mx(
+                out=sums[c][:],
+                lhsT=w_codes[:, g, :].bitcast(FP4X4),
+                lhsT_scale=w_scales[:, g, :],
+                rhs=h_codes[:].bitcast(FP8X4),
+                rhs_scale=h_scales[:],
+                start=(g == 0),
+                stop=(g == PASSES - 1),
+            )
+
+        steps = [(g, c) for g in range(PASSES) for c in range(CHUNKS)]
+        turn_pass(0)
+        for s in range(len(steps) + LAG):
+            if s < len(steps):
+                g, c = steps[s]
+                if c == 0 and g + 1 < PASSES:
+                    turn_pass(g + 1)
+                add_and_relu(g, c)
+            if s >= LAG:
+                quantise_and_multiply(*steps[s - LAG])
+
+        received = keep.tile([P, NODE_ROWS], F32, name="received")
+        for c in range(CHUNKS):
+            msg = work.tile([P, CHUNK_PAIRS], F32, name="msg")
+            nc.scalar.activation(
+                out=msg[:], in_=sums[c][:], func=ACT.Relu, bias=mb2_col[:, 0:1], scale=1.0
+            )
+            shape = [P, CHUNK_GRAPHS, NODES, NODES]
+            mask_view = (
+                mask_all[:, c * CHUNK_NODES : (c + 1) * CHUNK_NODES]
+                .rearrange("p (b j) -> p b j", b=CHUNK_GRAPHS)
+                .unsqueeze(2)
+                .to_broadcast(shape)
+            )
+            masked = work.tile([P, CHUNK_PAIRS], F32, name="masked")
+            nc.vector.tensor_tensor(
+                out=masked[:].rearrange("p (b i j) -> p b i j", b=CHUNK_GRAPHS, i=NODES),
+                in0=msg[:].rearrange("p (b i j) -> p b i j", b=CHUNK_GRAPHS, i=NODES),
+                in1=mask_view,
+                op=MULT,
+            )
+            nc.vector.tensor_reduce(
+                out=received[:, c * CHUNK_NODES : (c + 1) * CHUNK_NODES],
+                in_=masked[:].rearrange("p (r j) -> p r j", j=NODES),
+                axis=mybir.AxisListType.X,
+                op=ADD,
+            )
+        out_ps = turn_ps.tile([P, D_OUT], F32, name="out_ps", tag="turned_j")
+        nc.tensor.transpose(out_ps[:], received[:], ident_f32[:])
+        out_sb = keep.tile([P, D_OUT], F32, name="out_sb")
+        nc.vector.tensor_copy(out=out_sb[:], in_=out_ps[:])
+        nc.sync.dma_start(out=out.rearrange("b n d -> (b n) d"), in_=out_sb[:])

@@ -12,6 +12,7 @@ FP8X4 = mybir.dt.float8_e4m3fn_x4
 FP4X4 = mybir.dt.float4_e2m1fn_x4
 ADD = mybir.AluOpType.add
 MULT = mybir.AluOpType.mult
+MAX = mybir.AluOpType.max
 ACT = mybir.ActivationFunctionType
 
 P = 128
@@ -29,7 +30,7 @@ CHUNK_NODES = CHUNK_GRAPHS * NODES
 CHUNKS = GRAPHS // CHUNK_GRAPHS
 LOAD_PASSES = 4
 LOAD_COLS = LOAD_PASSES * K_PASS
-LAG = 2
+VECTOR_CHUNKS = 3
 
 FLOPS = 2 * GRAPHS * NODES * NODES * HIDDEN * D_OUT
 
@@ -43,6 +44,8 @@ def tile_graphdynamics_pa_k_kernel(
         loads = stack.enter_context(tc.tile_pool(name="loads", bufs=3))
         turned_sb = stack.enter_context(tc.tile_pool(name="turned_sb", bufs=2))
         work = stack.enter_context(tc.tile_pool(name="work", bufs=4))
+        gpsimd_work = stack.enter_context(tc.tile_pool(name="gpsimd_work", bufs=1))
+        stack.enter_context(tc.manual_schedule())
         sums_ps = stack.enter_context(tc.psum_pool(name="sums_ps", bufs=1))
         turn_ps = stack.enter_context(tc.psum_pool(name="turn_ps", bufs=2))
 
@@ -133,40 +136,59 @@ def tile_graphdynamics_pa_k_kernel(
                     xj_words[:, local * words + u : (local + 1) * words : 2],
                     ident_f32[:],
                 )
-            turned[g] = (recv, turned_j)
+            send_sb = turned_sb.tile([P, CHUNK_NODES * PACK], BF16, name="send_sb")
+            nc.scalar.copy(
+                out=send_sb[:],
+                in_=turned_j[:].rearrange("p r u -> p (r u)").bitcast(BF16)[
+                    :, VECTOR_CHUNKS * CHUNK_NODES * PACK :
+                ],
+            )
+            turned[g] = (recv, turned_j, send_sb)
 
         hidden = {}
 
-        def add_and_relu(g, c):
-            recv, turned_j = turned[g]
-            shape = [P, CHUNK_GRAPHS, NODES, NODES, PACK]
-            recv_view = (
+        pair_shape = [P, CHUNK_GRAPHS, NODES, NODES, PACK]
+
+        def receivers(recv, c):
+            return (
                 recv[:, :, c * CHUNK_NODES : (c + 1) * CHUNK_NODES]
                 .rearrange("p t (b i) -> p b i t", b=CHUNK_GRAPHS)
                 .unsqueeze(3)
-                .to_broadcast(shape)
+                .to_broadcast(pair_shape)
             )
-            send_view = (
-                turned_j[:]
-                .rearrange("p r u -> p (r u)")
-                .bitcast(BF16)
-                .rearrange("p (b j t) -> p b j t", b=GRAPHS, j=NODES)[
-                    :, c * CHUNK_GRAPHS : (c + 1) * CHUNK_GRAPHS
-                ]
+
+        def senders(send):
+            return (
+                send.rearrange("p (b j t) -> p b j t", b=CHUNK_GRAPHS, j=NODES)
                 .unsqueeze(2)
-                .to_broadcast(shape)
+                .to_broadcast(pair_shape)
             )
+
+        def pairs(flat):
+            return flat.rearrange("p (b i j t) -> p b i j t", b=CHUNK_GRAPHS, i=NODES, j=NODES)
+
+        def hidden_on_vector_and_scalar(g, c):
+            recv, turned_j, send_sb = turned[g]
+            send = turned_j[:].rearrange("p r u -> p (r u)").bitcast(BF16)[
+                :, c * CHUNK_NODES * PACK : (c + 1) * CHUNK_NODES * PACK
+            ]
             pre = work.tile([P, CHUNK_PAIRS * PACK], BF16, name="pre")
             nc.vector.tensor_tensor(
-                out=pre[:].rearrange(
-                    "p (b i j t) -> p b i j t", b=CHUNK_GRAPHS, i=NODES, j=NODES
-                ),
-                in0=recv_view,
-                in1=send_view,
-                op=ADD,
+                out=pairs(pre[:]), in0=receivers(recv, c), in1=senders(send), op=ADD
             )
             h = work.tile([P, CHUNK_PAIRS * PACK], BF16, name="h", align_bytes=64)
             nc.scalar.activation(out=h[:], in_=pre[:], func=ACT.Relu)
+            hidden[(g, c)] = h
+
+        def hidden_on_gpsimd(g, c):
+            recv, turned_j, send_sb = turned[g]
+            h = gpsimd_work.tile([P, CHUNK_PAIRS * PACK], BF16, name="h_gpsimd", align_bytes=64)
+            nc.gpsimd.tensor_tensor(
+                out=pairs(h[:]), in0=receivers(recv, c), in1=senders(send_sb[:]), op=ADD
+            )
+            nc.gpsimd.tensor_scalar(
+                out=h[:], in0=h[:], scalar1=0.0, scalar2=0.0, op0=MAX, op1=ADD
+            )
             hidden[(g, c)] = h
 
         def quantise_and_multiply(g, c):
@@ -184,16 +206,19 @@ def tile_graphdynamics_pa_k_kernel(
                 stop=(g == PASSES - 1),
             )
 
-        steps = [(g, c) for g in range(PASSES) for c in range(CHUNKS)]
         turn_pass(0)
-        for s in range(len(steps) + LAG):
-            if s < len(steps):
-                g, c = steps[s]
-                if c == 0 and g + 1 < PASSES:
-                    turn_pass(g + 1)
-                add_and_relu(g, c)
-            if s >= LAG:
-                quantise_and_multiply(*steps[s - LAG])
+        for g in range(PASSES + 1):
+            if g + 1 < PASSES:
+                turn_pass(g + 1)
+            if g < PASSES:
+                hidden_on_vector_and_scalar(g, 0)
+            if g > 0:
+                for c in range(CHUNKS):
+                    quantise_and_multiply(g - 1, c)
+            if g < PASSES:
+                hidden_on_gpsimd(g, VECTOR_CHUNKS)
+                for c in range(1, VECTOR_CHUNKS):
+                    hidden_on_vector_and_scalar(g, c)
 
         received = keep.tile([P, NODE_ROWS], F32, name="received")
         for c in range(CHUNKS):

@@ -12,7 +12,6 @@ FP8X4 = mybir.dt.float8_e4m3fn_x4
 FP4X4 = mybir.dt.float4_e2m1fn_x4
 ADD = mybir.AluOpType.add
 MULT = mybir.AluOpType.mult
-MAX = mybir.AluOpType.max
 ACT = mybir.ActivationFunctionType
 
 P = 128
@@ -186,13 +185,12 @@ def tile_graphdynamics_pa_k_kernel(
             nc.gpsimd.tensor_tensor(
                 out=pairs(h[:]), in0=receivers(recv, c), in1=senders(send_sb[:]), op=ADD
             )
-            nc.gpsimd.tensor_scalar(
-                out=h[:], in0=h[:], scalar1=0.0, scalar2=0.0, op0=MAX, op1=ADD
-            )
             hidden[(g, c)] = h
 
         def quantise_and_multiply(g, c):
             h = hidden[(g, c)]
+            if c >= VECTOR_CHUNKS:
+                nc.vector.tensor_scalar_max(out=h[:], in0=h[:], scalar1=0.0)
             h_codes = work.tile([P, CHUNK_PAIRS], U32, name="h_codes", align_bytes=64)
             h_scales = work.tile([P, CHUNK_PAIRS], U8, name="h_scales", align_bytes=64)
             nc.vector.quantize_mx(out=h_codes[:].bitcast(FP8X4), scales=h_scales[:], in_=h[:])

@@ -27,9 +27,11 @@ CHUNK_GRAPHS = 2
 CHUNK_PAIRS = CHUNK_GRAPHS * NODES * NODES
 CHUNK_NODES = CHUNK_GRAPHS * NODES
 CHUNKS = GRAPHS // CHUNK_GRAPHS
-LOAD_PASSES = 4
+LOAD_PASSES = 2
 LOAD_COLS = LOAD_PASSES * K_PASS
 VECTOR_CHUNKS = 3
+GRAPH_COLS = NODES * NODES * PACK
+CHUNK_COLS = CHUNK_PAIRS * PACK
 
 FLOPS = 2 * GRAPHS * NODES * NODES * HIDDEN * D_OUT
 
@@ -43,7 +45,7 @@ def tile_graphdynamics_pa_k_kernel(
         loads = stack.enter_context(tc.tile_pool(name="loads", bufs=3))
         turned_sb = stack.enter_context(tc.tile_pool(name="turned_sb", bufs=2))
         work = stack.enter_context(tc.tile_pool(name="work", bufs=4))
-        gpsimd_work = stack.enter_context(tc.tile_pool(name="gpsimd_work", bufs=1))
+        back_pool = stack.enter_context(tc.tile_pool(name="back_pool", bufs=1))
         stack.enter_context(tc.manual_schedule())
         sums_ps = stack.enter_context(tc.psum_pool(name="sums_ps", bufs=1))
         turn_ps = stack.enter_context(tc.psum_pool(name="turn_ps", bufs=2))
@@ -144,79 +146,92 @@ def tile_graphdynamics_pa_k_kernel(
             )
             turned[g] = (recv, turned_j, send_sb)
 
-        hidden = {}
-
-        pair_shape = [P, CHUNK_GRAPHS, NODES, NODES, PACK]
-
-        def receivers(recv, c):
+        def receivers(recv, first_graph, graphs):
             return (
-                recv[:, :, c * CHUNK_NODES : (c + 1) * CHUNK_NODES]
-                .rearrange("p t (b i) -> p b i t", b=CHUNK_GRAPHS)
+                recv[:, :, first_graph * NODES : (first_graph + graphs) * NODES]
+                .rearrange("p t (b i) -> p b i t", b=graphs)
                 .unsqueeze(3)
-                .to_broadcast(pair_shape)
+                .to_broadcast([P, graphs, NODES, NODES, PACK])
             )
 
-        def senders(send):
+        def senders(send, graphs):
             return (
-                send.rearrange("p (b j t) -> p b j t", b=CHUNK_GRAPHS, j=NODES)
+                send.rearrange("p (b j t) -> p b j t", b=graphs, j=NODES)
                 .unsqueeze(2)
-                .to_broadcast(pair_shape)
+                .to_broadcast([P, graphs, NODES, NODES, PACK])
             )
 
-        def pairs(flat):
-            return flat.rearrange("p (b i j t) -> p b i j t", b=CHUNK_GRAPHS, i=NODES, j=NODES)
+        def pairs(flat, graphs):
+            return flat.rearrange("p (b i j t) -> p b i j t", b=graphs, i=NODES, j=NODES)
 
-        def hidden_on_vector_and_scalar(g, c):
+        front = {}
+        back = {}
+
+        def hidden_on_vector_and_scalar(g, c, h):
             recv, turned_j, send_sb = turned[g]
             send = turned_j[:].rearrange("p r u -> p (r u)").bitcast(BF16)[
                 :, c * CHUNK_NODES * PACK : (c + 1) * CHUNK_NODES * PACK
             ]
-            pre = work.tile([P, CHUNK_PAIRS * PACK], BF16, name="pre")
+            pre = work.tile([P, CHUNK_COLS], BF16, name="pre")
             nc.vector.tensor_tensor(
-                out=pairs(pre[:]), in0=receivers(recv, c), in1=senders(send), op=ADD
+                out=pairs(pre[:], CHUNK_GRAPHS),
+                in0=receivers(recv, c * CHUNK_GRAPHS, CHUNK_GRAPHS),
+                in1=senders(send, CHUNK_GRAPHS),
+                op=ADD,
             )
-            h = work.tile([P, CHUNK_PAIRS * PACK], BF16, name="h", align_bytes=64)
-            nc.scalar.activation(out=h[:], in_=pre[:], func=ACT.Relu)
-            hidden[(g, c)] = h
+            nc.scalar.activation(out=h, in_=pre[:], func=ACT.Relu)
 
-        def hidden_on_gpsimd(g, c):
+        def add_on_gpsimd(g, h):
             recv, turned_j, send_sb = turned[g]
-            h = gpsimd_work.tile([P, CHUNK_PAIRS * PACK], BF16, name="h_gpsimd", align_bytes=64)
-            nc.gpsimd.tensor_tensor(
-                out=pairs(h[:]), in0=receivers(recv, c), in1=senders(send_sb[:]), op=ADD
-            )
-            hidden[(g, c)] = h
+            for b in range(CHUNK_GRAPHS):
+                nc.gpsimd.tensor_tensor(
+                    out=pairs(h[:, b * GRAPH_COLS : (b + 1) * GRAPH_COLS], 1),
+                    in0=receivers(recv, VECTOR_CHUNKS * CHUNK_GRAPHS + b, 1),
+                    in1=senders(send_sb[:, b * NODES * PACK : (b + 1) * NODES * PACK], 1),
+                    op=ADD,
+                )
 
-        def quantise_and_multiply(g, c):
-            h = hidden[(g, c)]
-            if c >= VECTOR_CHUNKS:
-                nc.vector.tensor_scalar_max(out=h[:], in0=h[:], scalar1=0.0)
-            h_codes = work.tile([P, CHUNK_PAIRS], U32, name="h_codes", align_bytes=64)
-            h_scales = work.tile([P, CHUNK_PAIRS], U8, name="h_scales", align_bytes=64)
+        def quantise_and_multiply(g, h, first_chunk):
+            h_codes = work.tile([P, 2 * CHUNK_PAIRS], U32, name="h_codes", align_bytes=64)
+            h_scales = work.tile([P, 2 * CHUNK_PAIRS], U8, name="h_scales", align_bytes=64)
             nc.vector.quantize_mx(out=h_codes[:].bitcast(FP8X4), scales=h_scales[:], in_=h[:])
-            nc.tensor.matmul_mx(
-                out=sums[c][:],
-                lhsT=w_codes[:, g, :].bitcast(FP4X4),
-                lhsT_scale=w_scales[:, g, :],
-                rhs=h_codes[:].bitcast(FP8X4),
-                rhs_scale=h_scales[:],
-                start=(g == 0),
-                stop=(g == PASSES - 1),
-            )
+            for half in range(2):
+                cols = slice(half * CHUNK_PAIRS, (half + 1) * CHUNK_PAIRS)
+                nc.tensor.matmul_mx(
+                    out=sums[first_chunk + half][:],
+                    lhsT=w_codes[:, g, :].bitcast(FP4X4),
+                    lhsT_scale=w_scales[:, g, :],
+                    rhs=h_codes[:, cols].bitcast(FP8X4),
+                    rhs_scale=h_scales[:, cols],
+                    start=(g == 0),
+                    stop=(g == PASSES - 1),
+                )
 
+        gpsimd_cols = slice(CHUNK_COLS, 2 * CHUNK_COLS)
+        scalar_clamps = slice(CHUNK_COLS, CHUNK_COLS + GRAPH_COLS)
+        vector_clamps = slice(CHUNK_COLS + GRAPH_COLS, 2 * CHUNK_COLS)
         turn_pass(0)
         for g in range(PASSES + 1):
             if g + 1 < PASSES:
                 turn_pass(g + 1)
             if g < PASSES:
-                hidden_on_vector_and_scalar(g, 0)
+                front[g] = work.tile([P, 2 * CHUNK_COLS], BF16, name="front", align_bytes=64)
+                hidden_on_vector_and_scalar(g, 0, front[g][:, 0:CHUNK_COLS])
             if g > 0:
-                for c in range(CHUNKS):
-                    quantise_and_multiply(g - 1, c)
+                last = back[g - 1]
+                nc.vector.tensor_scalar_max(
+                    out=last[:, vector_clamps], in0=last[:, vector_clamps], scalar1=0.0
+                )
+                quantise_and_multiply(g - 1, front[g - 1], 0)
+                quantise_and_multiply(g - 1, last, 2)
             if g < PASSES:
-                hidden_on_gpsimd(g, VECTOR_CHUNKS)
-                for c in range(1, VECTOR_CHUNKS):
-                    hidden_on_vector_and_scalar(g, c)
+                back[g] = back_pool.tile([P, 2 * CHUNK_COLS], BF16, name="back", align_bytes=64)
+                add_on_gpsimd(g, back[g][:, gpsimd_cols])
+                hidden_on_vector_and_scalar(g, 1, front[g][:, CHUNK_COLS : 2 * CHUNK_COLS])
+                hidden_on_vector_and_scalar(g, 2, back[g][:, 0:CHUNK_COLS])
+                nc.scalar.activation(
+                    out=back[g][:, scalar_clamps], in_=back[g][:, scalar_clamps], func=ACT.Relu
+                )
 
         received = keep.tile([P, NODE_ROWS], F32, name="received")
         for c in range(CHUNKS):

@@ -25,13 +25,21 @@ PASSES = HIDDEN // K_PASS
 NODE_ROWS = GRAPHS * NODES
 CHUNK_GRAPHS = 2
 CHUNK_PAIRS = CHUNK_GRAPHS * NODES * NODES
-CHUNK_NODES = CHUNK_GRAPHS * NODES
 CHUNKS = GRAPHS // CHUNK_GRAPHS
 LOAD_PASSES = 2
 LOAD_COLS = LOAD_PASSES * K_PASS
-VECTOR_CHUNKS = 3
 GRAPH_COLS = NODES * NODES * PACK
-CHUNK_COLS = CHUNK_PAIRS * PACK
+HALF_GRAPHS = GRAPHS // 2
+HALF_COLS = HALF_GRAPHS * GRAPH_COLS
+SEND_COLS = NODES * PACK
+
+VECTOR_ADDS = ((0, 2), (2, 4), (4, 5))
+GPSIMD_FIRST = 5
+TENSOR_GRAPH = 7
+TENSOR_RECV = NODES // 2
+TENSOR_PAIRS = TENSOR_RECV * NODES
+OWN_PASSES = 8
+OWN_COLS = OWN_PASSES * K_PASS
 
 FLOPS = 2 * GRAPHS * NODES * NODES * HIDDEN * D_OUT
 
@@ -43,12 +51,14 @@ def tile_graphdynamics_pa_k_kernel(
     with ExitStack() as stack:
         keep = stack.enter_context(tc.tile_pool(name="keep", bufs=1))
         loads = stack.enter_context(tc.tile_pool(name="loads", bufs=3))
-        turned_sb = stack.enter_context(tc.tile_pool(name="turned_sb", bufs=2))
-        work = stack.enter_context(tc.tile_pool(name="work", bufs=4))
-        back_pool = stack.enter_context(tc.tile_pool(name="back_pool", bufs=1))
+        turned_sb = stack.enter_context(tc.tile_pool(name="turned_sb", bufs=3))
+        work = stack.enter_context(tc.tile_pool(name="work", bufs=3))
+        hidden = stack.enter_context(tc.tile_pool(name="hidden", bufs=2))
         stack.enter_context(tc.manual_schedule())
         sums_ps = stack.enter_context(tc.psum_pool(name="sums_ps", bufs=1))
-        turn_ps = stack.enter_context(tc.psum_pool(name="turn_ps", bufs=2))
+        turn_i_ps = stack.enter_context(tc.psum_pool(name="turn_i_ps", bufs=1))
+        turn_j_ps = stack.enter_context(tc.psum_pool(name="turn_j_ps", bufs=2))
+        own_ps = stack.enter_context(tc.psum_pool(name="own_ps", bufs=1))
 
         xi_rows = xi_p.rearrange("b n h -> (b n) h")
         xj_rows = xj_p.rearrange("b n h -> (b n) h")
@@ -69,6 +79,32 @@ def tile_graphdynamics_pa_k_kernel(
         ident_f32 = keep.tile([P, P], F32, name="ident_f32")
         make_identity(nc, ident_f32[:])
 
+        mb1_rows = keep.tile([P, K_PASS], BF16, name="mb1_rows")
+        nc.vector.memset(mb1_rows[:], 0.0)
+        nc.scalar.dma_start(out=mb1_rows[0:PASSES, :], in_=mb1.rearrange("(g c) -> g c", c=K_PASS))
+        mb2_rows = keep.tile([P, D_OUT], BF16, name="mb2_rows")
+        nc.vector.memset(mb2_rows[:], 0.0)
+        nc.scalar.dma_start(out=mb2_rows[0:1, :], in_=mb2.rearrange("(o d) -> o d", o=1))
+
+        own_tiles = []
+        for o in range(2):
+            own = keep.tile([P, OWN_COLS], BF16, name="own%d" % o)
+            nc.vector.memset(own[:], 0.0)
+            own_tiles.append(own)
+        graph_rows = slice(TENSOR_GRAPH * NODES, (TENSOR_GRAPH + 1) * NODES)
+
+        def load_own(group):
+            own = own_tiles[group % 2]
+            cols = slice(group * OWN_COLS, (group + 1) * OWN_COLS)
+            nc.sync.dma_start(out=own[0:NODES, :], in_=xi_rows[graph_rows, cols])
+            nc.sync.dma_start(out=own[NODES : 2 * NODES, :], in_=xj_rows[graph_rows, cols])
+            nc.sync.dma_start(
+                out=own[2 * NODES : 2 * NODES + 1, :],
+                in_=mb1[cols].rearrange("(o c) -> o c", o=1),
+            )
+
+        load_own(0)
+
         w_scales = keep.tile([P, PASSES, D_OUT], U8, name="w_scales", align_bytes=64)
         nc.vector.memset(w_scales[:].bitcast(I32), 0)
         scale_words = mw2_scales.bitcast(I32)
@@ -81,18 +117,12 @@ def tile_graphdynamics_pa_k_kernel(
         nc.sync.dma_start(
             out=w_codes[:].bitcast(I32), in_=mw2_words.bitcast(I32).rearrange("g p c -> p g c")
         )
-
-        mb1_rows = keep.tile([P, K_PASS], BF16, name="mb1_rows")
-        nc.vector.memset(mb1_rows[:], 0.0)
-        nc.scalar.dma_start(out=mb1_rows[0:PASSES, :], in_=mb1.rearrange("(g c) -> g c", c=K_PASS))
-        mb2_rows = keep.tile([P, D_OUT], BF16, name="mb2_rows")
-        nc.vector.memset(mb2_rows[:], 0.0)
-        nc.scalar.dma_start(out=mb2_rows[0:1, :], in_=mb2.rearrange("(o d) -> o d", o=1))
+        load_own(1)
         mask_all = keep.tile([P, NODE_ROWS], BF16, name="mask_all")
         nc.scalar.dma_start(
             out=mask_all[:], in_=node_mask.rearrange("b n -> (b n)").partition_broadcast(P)
         )
-        bias_ps = turn_ps.tile([P, PACK + 1, P], BF16, name="bias_ps", tag="turned_i")
+        bias_ps = turn_i_ps.tile([P, PACK + 1, P], BF16, name="bias_ps", tag="turned_i")
         for t in range(PACK):
             nc.tensor.transpose(bias_ps[:, t, :], mb1_rows[:, t:K_PASS:PACK], ident_bf[:])
         nc.tensor.transpose(bias_ps[:, PACK, :], mb2_rows[:], ident_bf[:])
@@ -100,6 +130,23 @@ def tile_graphdynamics_pa_k_kernel(
         nc.vector.tensor_copy(out=mb1_col[:], in_=bias_ps[:, 0:PACK, 0:PASSES])
         mb2_col = keep.tile([P, 1], F32, name="mb2_col")
         nc.vector.tensor_copy(out=mb2_col[:], in_=bias_ps[:, PACK, 0:1])
+
+        first_recv = NODES - TENSOR_RECV
+        pair_shape = [P, TENSOR_RECV, NODES]
+        select_x = keep.tile([P, TENSOR_PAIRS], BF16, name="select_x")
+        nc.vector.tensor_tensor(
+            out=select_x[:].rearrange("p (i j) -> p i j", j=NODES),
+            in0=ident_bf[:, first_recv:NODES].unsqueeze(2).to_broadcast(pair_shape),
+            in1=ident_bf[:, NODES : 2 * NODES].unsqueeze(1).to_broadcast(pair_shape),
+            op=ADD,
+        )
+        select = keep.tile([P, TENSOR_PAIRS], BF16, name="select")
+        nc.vector.tensor_tensor(
+            out=select[:],
+            in0=select_x[:],
+            in1=ident_bf[:, 2 * NODES : 2 * NODES + 1].to_broadcast([P, TENSOR_PAIRS]),
+            op=ADD,
+        )
 
         sums = [
             sums_ps.tile([P, CHUNK_PAIRS], F32, name="sums%d" % c) for c in range(CHUNKS)
@@ -112,7 +159,7 @@ def tile_graphdynamics_pa_k_kernel(
             if local == 0 and group + 1 < PASSES // LOAD_PASSES:
                 load_x(group + 1)
             xi_sb, xj_sb = x_tiles[group]
-            turned_i = turn_ps.tile([P, PACK, NODE_ROWS], BF16, name="turned_i")
+            turned_i = turn_i_ps.tile([P, PACK, NODE_ROWS], BF16, name="turned_i")
             for t in range(PACK):
                 nc.tensor.transpose(
                     turned_i[:, t, :],
@@ -130,75 +177,102 @@ def tile_graphdynamics_pa_k_kernel(
                 )
             words = K_PASS // 2
             xj_words = xj_sb[:].bitcast(F32)
-            turned_j = turn_ps.tile([P, NODE_ROWS, 2], F32, name="turned_j")
+            turned_j = turn_j_ps.tile([P, NODE_ROWS, 2], F32, name="turned_j")
             for u in range(2):
                 nc.tensor.transpose(
                     turned_j[:, :, u],
                     xj_words[:, local * words + u : (local + 1) * words : 2],
                     ident_f32[:],
                 )
-            send_sb = turned_sb.tile([P, CHUNK_NODES * PACK], BF16, name="send_sb")
-            nc.scalar.copy(
-                out=send_sb[:],
-                in_=turned_j[:].rearrange("p r u -> p (r u)").bitcast(BF16)[
-                    :, VECTOR_CHUNKS * CHUNK_NODES * PACK :
-                ],
-            )
-            turned[g] = (recv, turned_j, send_sb)
+            send = turned_j[:].rearrange("p r u -> p (r u)").bitcast(BF16)
+            send_sb = turned_sb.tile([P, (GRAPHS - GPSIMD_FIRST) * SEND_COLS], BF16, name="send_sb")
+            nc.scalar.copy(out=send_sb[:], in_=send[:, GPSIMD_FIRST * SEND_COLS :])
+            turned[g] = (recv, send, send_sb)
 
-        def receivers(recv, first_graph, graphs):
+        def receivers(recv, first_row, graphs, rows):
             return (
-                recv[:, :, first_graph * NODES : (first_graph + graphs) * NODES]
+                recv[:, :, first_row : first_row + graphs * rows]
                 .rearrange("p t (b i) -> p b i t", b=graphs)
                 .unsqueeze(3)
-                .to_broadcast([P, graphs, NODES, NODES, PACK])
+                .to_broadcast([P, graphs, rows, NODES, PACK])
             )
 
-        def senders(send, graphs):
+        def senders(send, graphs, rows):
             return (
                 send.rearrange("p (b j t) -> p b j t", b=graphs, j=NODES)
                 .unsqueeze(2)
-                .to_broadcast([P, graphs, NODES, NODES, PACK])
+                .to_broadcast([P, graphs, rows, NODES, PACK])
             )
 
-        def pairs(flat, graphs):
-            return flat.rearrange("p (b i j t) -> p b i j t", b=graphs, i=NODES, j=NODES)
+        def pairs(flat, graphs, rows):
+            return flat.rearrange("p (b i j t) -> p b i j t", b=graphs, i=rows, j=NODES)
 
-        front = {}
-        back = {}
+        halves = {}
 
-        def hidden_on_vector_and_scalar(g, c, h):
-            recv, turned_j, send_sb = turned[g]
-            send = turned_j[:].rearrange("p r u -> p (r u)").bitcast(BF16)[
-                :, c * CHUNK_NODES * PACK : (c + 1) * CHUNK_NODES * PACK
-            ]
-            pre = work.tile([P, CHUNK_COLS], BF16, name="pre")
+        def columns(g, first_col, last_col):
+            half = first_col // HALF_COLS
+            return halves[g][half][:, first_col - half * HALF_COLS : last_col - half * HALF_COLS]
+
+        def clamp_on_scalar(g, first_col, last_col):
+            h = columns(g, first_col, last_col)
+            nc.scalar.activation(out=h, in_=h, func=ACT.Relu)
+
+        def add_on_vector(g, first, last):
+            recv, send, send_sb = turned[g]
+            graphs = last - first
             nc.vector.tensor_tensor(
-                out=pairs(pre[:], CHUNK_GRAPHS),
-                in0=receivers(recv, c * CHUNK_GRAPHS, CHUNK_GRAPHS),
-                in1=senders(send, CHUNK_GRAPHS),
+                out=pairs(columns(g, first * GRAPH_COLS, last * GRAPH_COLS), graphs, NODES),
+                in0=receivers(recv, first * NODES, graphs, NODES),
+                in1=senders(send[:, first * SEND_COLS : last * SEND_COLS], graphs, NODES),
                 op=ADD,
             )
-            nc.scalar.activation(out=h, in_=pre[:], func=ACT.Relu)
 
-        def add_on_gpsimd(g, h):
-            recv, turned_j, send_sb = turned[g]
-            for b in range(CHUNK_GRAPHS):
+        def add_on_gpsimd(g):
+            recv, send, send_sb = turned[g]
+            for b in range(GPSIMD_FIRST, GRAPHS):
+                rows = NODES - TENSOR_RECV if b == TENSOR_GRAPH else NODES
+                first_col = b * GRAPH_COLS
+                local = b - GPSIMD_FIRST
                 nc.gpsimd.tensor_tensor(
-                    out=pairs(h[:, b * GRAPH_COLS : (b + 1) * GRAPH_COLS], 1),
-                    in0=receivers(recv, VECTOR_CHUNKS * CHUNK_GRAPHS + b, 1),
-                    in1=senders(send_sb[:, b * NODES * PACK : (b + 1) * NODES * PACK], 1),
+                    out=pairs(columns(g, first_col, first_col + rows * SEND_COLS), 1, rows),
+                    in0=receivers(recv, b * NODES, 1, rows),
+                    in1=senders(send_sb[:, local * SEND_COLS : (local + 1) * SEND_COLS], 1, rows),
                     op=ADD,
                 )
 
-        def quantise_and_multiply(g, h, first_chunk):
+        tensor_cols = GRAPHS * GRAPH_COLS - TENSOR_PAIRS * PACK
+
+        def add_on_tensor(g):
+            group, local = divmod(g, OWN_PASSES)
+            own = own_tiles[group % 2]
+            own_sums = own_ps.tile([P, PACK, TENSOR_PAIRS], F32, name="own_sums")
+            for t in range(PACK):
+                nc.tensor.matmul(
+                    own_sums[:, t, :],
+                    lhsT=own[:, local * K_PASS + t : (local + 1) * K_PASS : PACK],
+                    rhs=select[:],
+                    start=True,
+                    stop=True,
+                )
+            nc.scalar.activation(
+                out=columns(g, tensor_cols, GRAPHS * GRAPH_COLS).rearrange(
+                    "p (n t) -> p n t", t=PACK
+                ),
+                in_=own_sums[:].rearrange("p t n -> p n t"),
+                func=ACT.Relu,
+            )
+            if local == OWN_PASSES - 1 and group + 2 < PASSES // OWN_PASSES:
+                load_own(group + 2)
+
+        def quantise_and_multiply(g, half):
+            h = halves[g][half]
             h_codes = work.tile([P, 2 * CHUNK_PAIRS], U32, name="h_codes", align_bytes=64)
             h_scales = work.tile([P, 2 * CHUNK_PAIRS], U8, name="h_scales", align_bytes=64)
             nc.vector.quantize_mx(out=h_codes[:].bitcast(FP8X4), scales=h_scales[:], in_=h[:])
-            for half in range(2):
-                cols = slice(half * CHUNK_PAIRS, (half + 1) * CHUNK_PAIRS)
+            for c in range(2):
+                cols = slice(c * CHUNK_PAIRS, (c + 1) * CHUNK_PAIRS)
                 nc.tensor.matmul_mx(
-                    out=sums[first_chunk + half][:],
+                    out=sums[2 * half + c][:],
                     lhsT=w_codes[:, g, :].bitcast(FP4X4),
                     lhsT_scale=w_scales[:, g, :],
                     rhs=h_codes[:, cols].bitcast(FP8X4),
@@ -207,31 +281,27 @@ def tile_graphdynamics_pa_k_kernel(
                     stop=(g == PASSES - 1),
                 )
 
-        gpsimd_cols = slice(CHUNK_COLS, 2 * CHUNK_COLS)
-        scalar_clamps = slice(CHUNK_COLS, CHUNK_COLS + GRAPH_COLS)
-        vector_clamps = slice(CHUNK_COLS + GRAPH_COLS, 2 * CHUNK_COLS)
+        vector_clamps = (GPSIMD_FIRST * GRAPH_COLS, TENSOR_GRAPH * GRAPH_COLS)
         turn_pass(0)
         for g in range(PASSES + 1):
-            if g + 1 < PASSES:
-                turn_pass(g + 1)
             if g < PASSES:
-                front[g] = work.tile([P, 2 * CHUNK_COLS], BF16, name="front", align_bytes=64)
-                hidden_on_vector_and_scalar(g, 0, front[g][:, 0:CHUNK_COLS])
+                halves[g] = [
+                    hidden.tile([P, HALF_COLS], BF16, name="front", align_bytes=64),
+                    hidden.tile([P, HALF_COLS], BF16, name="back", align_bytes=64),
+                ]
+                add_on_gpsimd(g)
+                if g + 1 < PASSES:
+                    turn_pass(g + 1)
+                add_on_tensor(g)
+                for first, last in VECTOR_ADDS:
+                    add_on_vector(g, first, last)
+                    clamp_on_scalar(g, first * GRAPH_COLS, last * GRAPH_COLS)
+                clamp_on_scalar(g, TENSOR_GRAPH * GRAPH_COLS, tensor_cols)
             if g > 0:
-                last = back[g - 1]
-                nc.vector.tensor_scalar_max(
-                    out=last[:, vector_clamps], in0=last[:, vector_clamps], scalar1=0.0
-                )
-                quantise_and_multiply(g - 1, front[g - 1], 0)
-                quantise_and_multiply(g - 1, last, 2)
-            if g < PASSES:
-                back[g] = back_pool.tile([P, 2 * CHUNK_COLS], BF16, name="back", align_bytes=64)
-                add_on_gpsimd(g, back[g][:, gpsimd_cols])
-                hidden_on_vector_and_scalar(g, 1, front[g][:, CHUNK_COLS : 2 * CHUNK_COLS])
-                hidden_on_vector_and_scalar(g, 2, back[g][:, 0:CHUNK_COLS])
-                nc.scalar.activation(
-                    out=back[g][:, scalar_clamps], in_=back[g][:, scalar_clamps], func=ACT.Relu
-                )
+                clamped = columns(g - 1, vector_clamps[0], vector_clamps[1])
+                nc.vector.tensor_scalar_max(out=clamped, in0=clamped, scalar1=0.0)
+                quantise_and_multiply(g - 1, 0)
+                quantise_and_multiply(g - 1, 1)
 
         received = keep.tile([P, NODE_ROWS], F32, name="received")
         for c in range(CHUNKS):
@@ -241,7 +311,7 @@ def tile_graphdynamics_pa_k_kernel(
             )
             shape = [P, CHUNK_GRAPHS, NODES, NODES]
             mask_view = (
-                mask_all[:, c * CHUNK_NODES : (c + 1) * CHUNK_NODES]
+                mask_all[:, c * (CHUNK_GRAPHS * NODES) : (c + 1) * (CHUNK_GRAPHS * NODES)]
                 .rearrange("p (b j) -> p b j", b=CHUNK_GRAPHS)
                 .unsqueeze(2)
                 .to_broadcast(shape)
@@ -254,12 +324,12 @@ def tile_graphdynamics_pa_k_kernel(
                 op=MULT,
             )
             nc.vector.tensor_reduce(
-                out=received[:, c * CHUNK_NODES : (c + 1) * CHUNK_NODES],
+                out=received[:, c * (CHUNK_GRAPHS * NODES) : (c + 1) * (CHUNK_GRAPHS * NODES)],
                 in_=masked[:].rearrange("p (r j) -> p r j", j=NODES),
                 axis=mybir.AxisListType.X,
                 op=ADD,
             )
-        out_ps = turn_ps.tile([P, D_OUT], F32, name="out_ps", tag="turned_j")
+        out_ps = turn_j_ps.tile([P, D_OUT], F32, name="out_ps", tag="turned_j")
         nc.tensor.transpose(out_ps[:], received[:], ident_f32[:])
         out_sb = keep.tile([P, D_OUT], F32, name="out_sb")
         nc.vector.tensor_copy(out=out_sb[:], in_=out_ps[:])

@@ -34,10 +34,11 @@ HALF_COLS = HALF_GRAPHS * GRAPH_COLS
 SEND_COLS = NODES * PACK
 
 VECTOR_ADDS = ((0, 2), (2, 4), (4, 5))
-GPSIMD_FIRST = 5
+GPSIMD_GRAPHS = (5, 7)
 TENSOR_GRAPH = 7
-TENSOR_RECV = NODES // 2
-TENSOR_PAIRS = TENSOR_RECV * NODES
+HALF_RECV = NODES // 2
+HALF_PAIRS = HALF_RECV * NODES
+HALF_GRAPH_COLS = HALF_PAIRS * PACK
 OWN_PASSES = 8
 OWN_COLS = OWN_PASSES * K_PASS
 
@@ -131,20 +132,19 @@ def tile_graphdynamics_pa_k_kernel(
         mb2_col = keep.tile([P, 1], F32, name="mb2_col")
         nc.vector.tensor_copy(out=mb2_col[:], in_=bias_ps[:, PACK, 0:1])
 
-        first_recv = NODES - TENSOR_RECV
-        pair_shape = [P, TENSOR_RECV, NODES]
-        select_x = keep.tile([P, TENSOR_PAIRS], BF16, name="select_x")
+        pair_shape = [P, NODES, NODES]
+        select_x = keep.tile([P, 2 * HALF_PAIRS], BF16, name="select_x")
         nc.vector.tensor_tensor(
             out=select_x[:].rearrange("p (i j) -> p i j", j=NODES),
-            in0=ident_bf[:, first_recv:NODES].unsqueeze(2).to_broadcast(pair_shape),
+            in0=ident_bf[:, 0:NODES].unsqueeze(2).to_broadcast(pair_shape),
             in1=ident_bf[:, NODES : 2 * NODES].unsqueeze(1).to_broadcast(pair_shape),
             op=ADD,
         )
-        select = keep.tile([P, TENSOR_PAIRS], BF16, name="select")
+        select = keep.tile([P, 2 * HALF_PAIRS], BF16, name="select")
         nc.vector.tensor_tensor(
             out=select[:],
             in0=select_x[:],
-            in1=ident_bf[:, 2 * NODES : 2 * NODES + 1].to_broadcast([P, TENSOR_PAIRS]),
+            in1=ident_bf[:, 2 * NODES : 2 * NODES + 1].to_broadcast([P, 2 * HALF_PAIRS]),
             op=ADD,
         )
 
@@ -185,8 +185,9 @@ def tile_graphdynamics_pa_k_kernel(
                     ident_f32[:],
                 )
             send = turned_j[:].rearrange("p r u -> p (r u)").bitcast(BF16)
-            send_sb = turned_sb.tile([P, (GRAPHS - GPSIMD_FIRST) * SEND_COLS], BF16, name="send_sb")
-            nc.scalar.copy(out=send_sb[:], in_=send[:, GPSIMD_FIRST * SEND_COLS :])
+            first, last = GPSIMD_GRAPHS
+            send_sb = turned_sb.tile([P, (last - first) * SEND_COLS], BF16, name="send_sb")
+            nc.scalar.copy(out=send_sb[:], in_=send[:, first * SEND_COLS : last * SEND_COLS])
             turned[g] = (recv, send, send_sb)
 
         def receivers(recv, first_row, graphs, rows):
@@ -217,52 +218,49 @@ def tile_graphdynamics_pa_k_kernel(
             h = columns(g, first_col, last_col)
             nc.scalar.activation(out=h, in_=h, func=ACT.Relu)
 
-        def add_on_vector(g, first, last):
+        def add_on_vector(g, first, graphs, rows):
             recv, send, send_sb = turned[g]
-            graphs = last - first
+            first_col = first * GRAPH_COLS
             nc.vector.tensor_tensor(
-                out=pairs(columns(g, first * GRAPH_COLS, last * GRAPH_COLS), graphs, NODES),
-                in0=receivers(recv, first * NODES, graphs, NODES),
-                in1=senders(send[:, first * SEND_COLS : last * SEND_COLS], graphs, NODES),
+                out=pairs(columns(g, first_col, first_col + graphs * rows * SEND_COLS), graphs, rows),
+                in0=receivers(recv, first * NODES, graphs, rows),
+                in1=senders(send[:, first * SEND_COLS : (first + graphs) * SEND_COLS], graphs, rows),
                 op=ADD,
             )
 
         def add_on_gpsimd(g):
             recv, send, send_sb = turned[g]
-            for b in range(GPSIMD_FIRST, GRAPHS):
-                rows = NODES - TENSOR_RECV if b == TENSOR_GRAPH else NODES
-                first_col = b * GRAPH_COLS
-                local = b - GPSIMD_FIRST
+            first, last = GPSIMD_GRAPHS
+            for b in range(first, last):
+                local = b - first
                 nc.gpsimd.tensor_tensor(
-                    out=pairs(columns(g, first_col, first_col + rows * SEND_COLS), 1, rows),
-                    in0=receivers(recv, b * NODES, 1, rows),
-                    in1=senders(send_sb[:, local * SEND_COLS : (local + 1) * SEND_COLS], 1, rows),
+                    out=pairs(columns(g, b * GRAPH_COLS, (b + 1) * GRAPH_COLS), 1, NODES),
+                    in0=receivers(recv, b * NODES, 1, NODES),
+                    in1=senders(send_sb[:, local * SEND_COLS : (local + 1) * SEND_COLS], 1, NODES),
                     op=ADD,
                 )
 
-        tensor_cols = GRAPHS * GRAPH_COLS - TENSOR_PAIRS * PACK
+        half_cols = [TENSOR_GRAPH * GRAPH_COLS + half * HALF_GRAPH_COLS for half in range(3)]
 
-        def add_on_tensor(g):
+        def add_on_tensor(g, half):
             group, local = divmod(g, OWN_PASSES)
             own = own_tiles[group % 2]
-            own_sums = own_ps.tile([P, PACK, TENSOR_PAIRS], F32, name="own_sums")
+            own_sums = own_ps.tile([P, PACK, HALF_PAIRS], F32, name="own_sums")
             for t in range(PACK):
                 nc.tensor.matmul(
                     own_sums[:, t, :],
                     lhsT=own[:, local * K_PASS + t : (local + 1) * K_PASS : PACK],
-                    rhs=select[:],
+                    rhs=select[:, half * HALF_PAIRS : (half + 1) * HALF_PAIRS],
                     start=True,
                     stop=True,
                 )
             nc.scalar.activation(
-                out=columns(g, tensor_cols, GRAPHS * GRAPH_COLS).rearrange(
+                out=columns(g, half_cols[half], half_cols[half + 1]).rearrange(
                     "p (n t) -> p n t", t=PACK
                 ),
                 in_=own_sums[:].rearrange("p t n -> p n t"),
                 func=ACT.Relu,
             )
-            if local == OWN_PASSES - 1 and group + 2 < PASSES // OWN_PASSES:
-                load_own(group + 2)
 
         def quantise_and_multiply(g, half):
             h = halves[g][half]
@@ -281,7 +279,8 @@ def tile_graphdynamics_pa_k_kernel(
                     stop=(g == PASSES - 1),
                 )
 
-        vector_clamps = (GPSIMD_FIRST * GRAPH_COLS, TENSOR_GRAPH * GRAPH_COLS)
+        vector_clamps = (GPSIMD_GRAPHS[0] * GRAPH_COLS, (GPSIMD_GRAPHS[0] + 1) * GRAPH_COLS)
+        scalar_clamps = (vector_clamps[1], GPSIMD_GRAPHS[1] * GRAPH_COLS)
         turn_pass(0)
         for g in range(PASSES + 1):
             if g < PASSES:
@@ -292,11 +291,18 @@ def tile_graphdynamics_pa_k_kernel(
                 add_on_gpsimd(g)
                 if g + 1 < PASSES:
                     turn_pass(g + 1)
-                add_on_tensor(g)
+                add_on_tensor(g, 1)
                 for first, last in VECTOR_ADDS:
-                    add_on_vector(g, first, last)
+                    add_on_vector(g, first, last - first, NODES)
                     clamp_on_scalar(g, first * GRAPH_COLS, last * GRAPH_COLS)
-                clamp_on_scalar(g, TENSOR_GRAPH * GRAPH_COLS, tensor_cols)
+                if g % 2:
+                    add_on_tensor(g, 0)
+                else:
+                    add_on_vector(g, TENSOR_GRAPH, 1, HALF_RECV)
+                    clamp_on_scalar(g, half_cols[0], half_cols[1])
+                if g % OWN_PASSES == OWN_PASSES - 1 and g + OWN_PASSES + 1 < PASSES:
+                    load_own(g // OWN_PASSES + 2)
+                clamp_on_scalar(g, scalar_clamps[0], scalar_clamps[1])
             if g > 0:
                 clamped = columns(g - 1, vector_clamps[0], vector_clamps[1])
                 nc.vector.tensor_scalar_max(out=clamped, in0=clamped, scalar1=0.0)

from contextlib import ExitStack

import concourse.mybir as mybir
from concourse.masks import make_identity

F32 = mybir.dt.float32
BF16 = mybir.dt.bfloat16
I32 = mybir.dt.int32
U32 = mybir.dt.uint32
U8 = mybir.dt.uint8
FP8X4 = mybir.dt.float8_e4m3fn_x4
FP4X4 = mybir.dt.float4_e2m1fn_x4
ADD = mybir.AluOpType.add
MULT = mybir.AluOpType.mult
ACT = mybir.ActivationFunctionType

P = 128
PACK = 4
K_PASS = P * PACK
GRAPHS = 8
NODES = 16
HIDDEN = 16384
D_OUT = 128
PASSES = HIDDEN // K_PASS
NODE_ROWS = GRAPHS * NODES
CHUNK_GRAPHS = 2
CHUNK_PAIRS = CHUNK_GRAPHS * NODES * NODES
CHUNKS = GRAPHS // CHUNK_GRAPHS
LOAD_PASSES = 2
LOAD_COLS = LOAD_PASSES * K_PASS
GRAPH_COLS = NODES * NODES * PACK
HALF_GRAPHS = GRAPHS // 2
HALF_COLS = HALF_GRAPHS * GRAPH_COLS
SEND_COLS = NODES * PACK

VECTOR_ADDS = ((0, 2), (2, 4), (4, 5))
GPSIMD_GRAPHS = (5, 7)
TENSOR_GRAPH = 7
HALF_RECV = NODES // 2
HALF_PAIRS = HALF_RECV * NODES
HALF_GRAPH_COLS = HALF_PAIRS * PACK
OWN_PASSES = 8
OWN_COLS = OWN_PASSES * K_PASS

FLOPS = 2 * GRAPHS * NODES * NODES * HIDDEN * D_OUT


def tile_graphdynamics_pa_k_kernel(
    tc, xi_p, xj_p, node_mask, mb1, mw2_words, mw2_scales, mb2, out
):
    nc = tc.nc
    with ExitStack() as stack:
        keep = stack.enter_context(tc.tile_pool(name="keep", bufs=1))
        loads = stack.enter_context(tc.tile_pool(name="loads", bufs=3))
        turned_sb = stack.enter_context(tc.tile_pool(name="turned_sb", bufs=3))
        work = stack.enter_context(tc.tile_pool(name="work", bufs=3))
        hidden = stack.enter_context(tc.tile_pool(name="hidden", bufs=2))
        stack.enter_context(tc.manual_schedule())
        sums_ps = stack.enter_context(tc.psum_pool(name="sums_ps", bufs=1))
        turn_i_ps = stack.enter_context(tc.psum_pool(name="turn_i_ps", bufs=1))
        turn_j_ps = stack.enter_context(tc.psum_pool(name="turn_j_ps", bufs=2))
        own_ps = stack.enter_context(tc.psum_pool(name="own_ps", bufs=1))

        xi_rows = xi_p.rearrange("b n h -> (b n) h")
        xj_rows = xj_p.rearrange("b n h -> (b n) h")
        x_tiles = {}

        def load_x(group):
            cols = slice(group * LOAD_COLS, (group + 1) * LOAD_COLS)
            xi_sb = loads.tile([P, LOAD_COLS], BF16, name="xi_sb")
            nc.sync.dma_start(out=xi_sb[:], in_=xi_rows[:, cols])
            xj_sb = loads.tile([P, LOAD_COLS], BF16, name="xj_sb")
            nc.sync.dma_start(out=xj_sb[:], in_=xj_rows[:, cols])
            x_tiles[group] = (xi_sb, xj_sb)

        load_x(0)

        ident_bf = keep.tile([P, P], BF16, name="ident_bf")
        make_identity(nc, ident_bf[:])
        ident_f32 = keep.tile([P, P], F32, name="ident_f32")
        make_identity(nc, ident_f32[:])

        mb1_rows = keep.tile([P, K_PASS], BF16, name="mb1_rows")
        nc.vector.memset(mb1_rows[:], 0.0)
        nc.scalar.dma_start(out=mb1_rows[0:PASSES, :], in_=mb1.rearrange("(g c) -> g c", c=K_PASS))
        mb2_rows = keep.tile([P, D_OUT], BF16, name="mb2_rows")
        nc.vector.memset(mb2_rows[:], 0.0)
        nc.scalar.dma_start(out=mb2_rows[0:1, :], in_=mb2.rearrange("(o d) -> o d", o=1))

        own_tiles = []
        for o in range(2):
            own = keep.tile([P, OWN_COLS], BF16, name="own%d" % o)
            nc.vector.memset(own[:], 0.0)
            own_tiles.append(own)
        graph_rows = slice(TENSOR_GRAPH * NODES, (TENSOR_GRAPH + 1) * NODES)

        def load_own(group):
            own = own_tiles[group % 2]
            cols = slice(group * OWN_COLS, (group + 1) * OWN_COLS)
            nc.sync.dma_start(out=own[0:NODES, :], in_=xi_rows[graph_rows, cols])
            nc.sync.dma_start(out=own[NODES : 2 * NODES, :], in_=xj_rows[graph_rows, cols])
            nc.sync.dma_start(
                out=own[2 * NODES : 2 * NODES + 1, :],
                in_=mb1[cols].rearrange("(o c) -> o c", o=1),
            )

        load_own(0)

        w_scales = keep.tile([P, PASSES, D_OUT], U8, name="w_scales", align_bytes=64)
        nc.vector.memset(w_scales[:].bitcast(I32), 0)
        scale_words = mw2_scales.bitcast(I32)
        for quadrant in range(4):
            nc.sync.dma_start(
                out=w_scales[32 * quadrant : 32 * quadrant + 4].bitcast(I32),
                in_=scale_words[:, 4 * quadrant : 4 * quadrant + 4, :].rearrange("g r n -> r g n"),
            )
        w_codes = keep.tile([P, PASSES, 2 * D_OUT], U8, name="w_codes", align_bytes=64)
        nc.sync.dma_start(
            out=w_codes[:].bitcast(I32), in_=mw2_words.bitcast(I32).rearrange("g p c -> p g c")
        )
        load_own(1)
        mask_all = keep.tile([P, NODE_ROWS], BF16, name="mask_all")
        nc.scalar.dma_start(
            out=mask_all[:], in_=node_mask.rearrange("b n -> (b n)").partition_broadcast(P)
        )
        bias_ps = turn_i_ps.tile([P, PACK + 1, P], BF16, name="bias_ps", tag="turned_i")
        for t in range(PACK):
            nc.tensor.transpose(bias_ps[:, t, :], mb1_rows[:, t:K_PASS:PACK], ident_bf[:])
        nc.tensor.transpose(bias_ps[:, PACK, :], mb2_rows[:], ident_bf[:])
        mb1_col = keep.tile([P, PACK, PASSES], F32, name="mb1_col")
        nc.vector.tensor_copy(out=mb1_col[:], in_=bias_ps[:, 0:PACK, 0:PASSES])
        mb2_col = keep.tile([P, 1], F32, name="mb2_col")
        nc.vector.tensor_copy(out=mb2_col[:], in_=bias_ps[:, PACK, 0:1])

        pair_shape = [P, NODES, NODES]
        select_x = keep.tile([P, 2 * HALF_PAIRS], BF16, name="select_x")
        nc.vector.tensor_tensor(
            out=select_x[:].rearrange("p (i j) -> p i j", j=NODES),
            in0=ident_bf[:, 0:NODES].unsqueeze(2).to_broadcast(pair_shape),
            in1=ident_bf[:, NODES : 2 * NODES].unsqueeze(1).to_broadcast(pair_shape),
            op=ADD,
        )
        select = keep.tile([P, 2 * HALF_PAIRS], BF16, name="select")
        nc.vector.tensor_tensor(
            out=select[:],
            in0=select_x[:],
            in1=ident_bf[:, 2 * NODES : 2 * NODES + 1].to_broadcast([P, 2 * HALF_PAIRS]),
            op=ADD,
        )

        sums = [
            sums_ps.tile([P, CHUNK_PAIRS], F32, name="sums%d" % c) for c in range(CHUNKS)
        ]

        turned = {}

        def turn_pass(g):
            group, local = divmod(g, LOAD_PASSES)
            if local == 0 and group + 1 < PASSES // LOAD_PASSES:
                load_x(group + 1)
            xi_sb, xj_sb = x_tiles[group]
            turned_i = turn_i_ps.tile([P, PACK, NODE_ROWS], BF16, name="turned_i")
            for t in range(PACK):
                nc.tensor.transpose(
                    turned_i[:, t, :],
                    xi_sb[:, local * K_PASS + t : (local + 1) * K_PASS : PACK],
                    ident_bf[:],
                )
            recv = turned_sb.tile([P, PACK, NODE_ROWS], F32, name="recv")
            for t in range(PACK):
                nc.scalar.activation(
                    out=recv[:, t, :],
                    in_=turned_i[:, t, :],
                    func=ACT.Identity,
                    bias=mb1_col[:, t, g : g + 1],
                    scale=1.0,
                )
            words = K_PASS // 2
            xj_words = xj_sb[:].bitcast(F32)
            turned_j = turn_j_ps.tile([P, NODE_ROWS, 2], F32, name="turned_j")
            for u in range(2):
                nc.tensor.transpose(
                    turned_j[:, :, u],
                    xj_words[:, local * words + u : (local + 1) * words : 2],
                    ident_f32[:],
                )
            send = turned_j[:].rearrange("p r u -> p (r u)").bitcast(BF16)
            first, last = GPSIMD_GRAPHS
            send_sb = turned_sb.tile([P, (last - first) * SEND_COLS], BF16, name="send_sb")
            nc.scalar.copy(out=send_sb[:], in_=send[:, first * SEND_COLS : last * SEND_COLS])
            turned[g] = (recv, send, send_sb)

        def receivers(recv, first_row, graphs, rows):
            return (
                recv[:, :, first_row : first_row + graphs * rows]
                .rearrange("p t (b i) -> p b i t", b=graphs)
                .unsqueeze(3)
                .to_broadcast([P, graphs, rows, NODES, PACK])
            )

        def senders(send, graphs, rows):
            return (
                send.rearrange("p (b j t) -> p b j t", b=graphs, j=NODES)
                .unsqueeze(2)
                .to_broadcast([P, graphs, rows, NODES, PACK])
            )

        def pairs(flat, graphs, rows):
            return flat.rearrange("p (b i j t) -> p b i j t", b=graphs, i=rows, j=NODES)

        halves = {}

        def columns(g, first_col, last_col):
            half = first_col // HALF_COLS
            return halves[g][half][:, first_col - half * HALF_COLS : last_col - half * HALF_COLS]

        def clamp_on_scalar(g, first_col, last_col):
            h = columns(g, first_col, last_col)
            nc.scalar.activation(out=h, in_=h, func=ACT.Relu)

        def add_on_vector(g, first, graphs, rows):
            recv, send, send_sb = turned[g]
            first_col = first * GRAPH_COLS
            nc.vector.tensor_tensor(
                out=pairs(columns(g, first_col, first_col + graphs * rows * SEND_COLS), graphs, rows),
                in0=receivers(recv, first * NODES, graphs, rows),
                in1=senders(send[:, first * SEND_COLS : (first + graphs) * SEND_COLS], graphs, rows),
                op=ADD,
            )

        def add_on_gpsimd(g):
            recv, send, send_sb = turned[g]
            first, last = GPSIMD_GRAPHS
            for b in range(first, last):
                local = b - first
                nc.gpsimd.tensor_tensor(
                    out=pairs(columns(g, b * GRAPH_COLS, (b + 1) * GRAPH_COLS), 1, NODES),
                    in0=receivers(recv, b * NODES, 1, NODES),
                    in1=senders(send_sb[:, local * SEND_COLS : (local + 1) * SEND_COLS], 1, NODES),
                    op=ADD,
                )

        half_cols = [TENSOR_GRAPH * GRAPH_COLS + half * HALF_GRAPH_COLS for half in range(3)]

        def add_on_tensor(g, half):
            group, local = divmod(g, OWN_PASSES)
            own = own_tiles[group % 2]
            own_sums = own_ps.tile([P, PACK, HALF_PAIRS], F32, name="own_sums")
            for t in range(PACK):
                nc.tensor.matmul(
                    own_sums[:, t, :],
                    lhsT=own[:, local * K_PASS + t : (local + 1) * K_PASS : PACK],
                    rhs=select[:, half * HALF_PAIRS : (half + 1) * HALF_PAIRS],
                    start=True,
                    stop=True,
                )
            nc.scalar.activation(
                out=columns(g, half_cols[half], half_cols[half + 1]).rearrange(
                    "p (n t) -> p n t", t=PACK
                ),
                in_=own_sums[:].rearrange("p t n -> p n t"),
                func=ACT.Relu,
            )

        def quantise_and_multiply(g, half):
            h = halves[g][half]
            h_codes = work.tile([P, 2 * CHUNK_PAIRS], U32, name="h_codes", align_bytes=64)
            h_scales = work.tile([P, 2 * CHUNK_PAIRS], U8, name="h_scales", align_bytes=64)
            nc.vector.quantize_mx(out=h_codes[:].bitcast(FP8X4), scales=h_scales[:], in_=h[:])
            for c in range(2):
                cols = slice(c * CHUNK_PAIRS, (c + 1) * CHUNK_PAIRS)
                nc.tensor.matmul_mx(
                    out=sums[2 * half + c][:],
                    lhsT=w_codes[:, g, :].bitcast(FP4X4),
                    lhsT_scale=w_scales[:, g, :],
                    rhs=h_codes[:, cols].bitcast(FP8X4),
                    rhs_scale=h_scales[:, cols],
                    start=(g == 0),
                    stop=(g == PASSES - 1),
                )

        vector_clamps = (GPSIMD_GRAPHS[0] * GRAPH_COLS, (GPSIMD_GRAPHS[0] + 1) * GRAPH_COLS)
        scalar_clamps = (vector_clamps[1], GPSIMD_GRAPHS[1] * GRAPH_COLS)
        turn_pass(0)
        for g in range(PASSES + 1):
            if g < PASSES:
                halves[g] = [
                    hidden.tile([P, HALF_COLS], BF16, name="front", align_bytes=64),
                    hidden.tile([P, HALF_COLS], BF16, name="back", align_bytes=64),
                ]
                add_on_gpsimd(g)
                if g + 1 < PASSES:
                    turn_pass(g + 1)
                add_on_tensor(g, 1)
                for first, last in VECTOR_ADDS:
                    add_on_vector(g, first, last - first, NODES)
                    clamp_on_scalar(g, first * GRAPH_COLS, last * GRAPH_COLS)
                if g % 2:
                    add_on_tensor(g, 0)
                else:
                    add_on_vector(g, TENSOR_GRAPH, 1, HALF_RECV)
                    clamp_on_scalar(g, half_cols[0], half_cols[1])
                if g % OWN_PASSES == OWN_PASSES - 1 and g + OWN_PASSES + 1 < PASSES:
                    load_own(g // OWN_PASSES + 2)
                clamp_on_scalar(g, scalar_clamps[0], scalar_clamps[1])
            if g > 0:
                clamped = columns(g - 1, vector_clamps[0], vector_clamps[1])
                nc.vector.tensor_scalar_max(out=clamped, in0=clamped, scalar1=0.0)
                quantise_and_multiply(g - 1, 0)
                quantise_and_multiply(g - 1, 1)

        received = keep.tile([P, NODE_ROWS], F32, name="received")
        for c in range(CHUNKS):
            msg = work.tile([P, CHUNK_PAIRS], F32, name="msg")
            nc.scalar.activation(
                out=msg[:], in_=sums[c][:], func=ACT.Relu, bias=mb2_col[:, 0:1], scale=1.0
            )
            shape = [P, CHUNK_GRAPHS, NODES, NODES]
            mask_view = (
                mask_all[:, c * (CHUNK_GRAPHS * NODES) : (c + 1) * (CHUNK_GRAPHS * NODES)]
                .rearrange("p (b j) -> p b j", b=CHUNK_GRAPHS)
                .unsqueeze(2)
                .to_broadcast(shape)
            )
            masked = work.tile([P, CHUNK_PAIRS], F32, name="masked")
            nc.vector.tensor_tensor(
                out=masked[:].rearrange("p (b i j) -> p b i j", b=CHUNK_GRAPHS, i=NODES),
                in0=msg[:].rearrange("p (b i j) -> p b i j", b=CHUNK_GRAPHS, i=NODES),
                in1=mask_view,
                op=MULT,
            )
            nc.vector.tensor_reduce(
                out=received[:, c * (CHUNK_GRAPHS * NODES) : (c + 1) * (CHUNK_GRAPHS * NODES)],
                in_=masked[:].rearrange("p (r j) -> p r j", j=NODES),
                axis=mybir.AxisListType.X,
                op=ADD,
            )
        out_ps = turn_j_ps.tile([P, D_OUT], F32, name="out_ps", tag="turned_j")
        nc.tensor.transpose(out_ps[:], received[:], ident_f32[:])
        out_sb = keep.tile([P, D_OUT], F32, name="out_sb")
        nc.vector.tensor_copy(out=out_sb[:], in_=out_ps[:])
        nc.sync.dma_start(out=out.rearrange("b n d -> (b n) d"), in_=out_sb[:])
